import numpy as np
import ml_dtypes


def mxq(x, axis, fmt="e4m3"):
    dtype, down = {"e4m3": (ml_dtypes.float8_e4m3fn, 7), "e5m2": (ml_dtypes.float8_e5m2, 14)}[fmt]
    v = np.moveaxis(np.asarray(x, np.float32).astype(ml_dtypes.bfloat16).astype(np.float64), axis, -1)
    blocks = v.reshape(v.shape[:-1] + (-1, 32))
    amax = np.abs(blocks).max(-1, keepdims=True)
    byte = np.maximum(np.where(amax > 0, np.frexp(amax)[1] - 1 + 127, 0) - down, 1)
    scale = np.exp2(byte - 127.0)
    codes = (blocks / scale).astype(np.float32).astype(dtype).astype(np.float64)
    return np.moveaxis((codes * scale).reshape(v.shape), -1, axis)


WIDE = False


def mx_kscale(k):
    if not WIDE:
        return np.ones(k)
    levels = np.array([20, -20, 10, -10, 0])
    a = np.random.permutation(np.resize(levels, k // 512 * 4)).reshape(k // 512, 4)
    idx = np.arange(k)
    return np.exp2(a[idx // 512, idx % 128 // 32])


BF16 = ml_dtypes.bfloat16


def bf(x):
    return np.asarray(x, np.float32).astype(BF16)


def f64(x):
    return np.asarray(x).astype(np.float64)


B, HW, C, HID, WS, SS, HEADS = 1, 32, 1024, 2048, 8, 4, 16
L = HW * HW
NH = HW // WS
EPS = 1e-5
NW = NH * NH * B
T = NW * WS * WS


def from_windows(v):
    k = v.shape[-1]
    v = np.swapaxes(v.reshape(B, NH, NH, WS, WS, k), 2, 3).reshape(B, HW, HW, k)
    return np.roll(v, (SS, SS), axis=(1, 2)).reshape(B, L, k)


def to_windows(v):
    k = v.shape[-1]
    v = np.roll(v.reshape(B, HW, HW, k), (-SS, -SS), axis=(1, 2))
    return np.swapaxes(v.reshape(B, NH, WS, NH, WS, k), 2, 3).reshape(NW, WS * WS, k)


def setup_inputs():
    s = np.asarray(mx_kscale(T)).reshape(NW, WS * WS, 1)
    o0 = bf(0.4 * np.random.standard_normal((NW, WS * WS, C)))
    out_w = bf(np.random.standard_normal((C, C)) / np.sqrt(C))
    out_b = bf(0.1 * np.random.standard_normal(C))
    ada1_scale = bf(1.0 + 0.1 * np.random.standard_normal((1, L, 1)))
    ada1_shift = bf(0.1 * np.random.standard_normal((1, L, 1)))
    x = bf(np.random.standard_normal((B, L, C)))
    g = bf(np.random.standard_normal((B, L, C)) * np.exp2(np.random.randint(-12, 1, (B, L, 1))) / from_windows(s))
    a = f64(o0) @ f64(out_w).T + f64(out_b)
    return {"o_attn": bf(f64(o0) * s), "out_w": out_w, "out_b": out_b, "ada1_scale": ada1_scale,
            "ada1_shift": ada1_shift, "x": x, "a": np.asarray(a, np.float32), "grad_out": g}


def reference(o_attn, out_w, out_b, ada1_scale, ada1_shift, x, a, grad_out):
    g = to_windows(f64(grad_out) * f64(ada1_scale)).reshape(T, C)
    af = f64(a).reshape(T, C)
    c = af - af.mean(1, keepdims=True)
    sd = np.sqrt((c * c).sum(1, keepdims=True) / (C - 1))
    r = 1.0 / (sd + EPS)
    p = (g * c).sum(1, keepdims=True)
    da = r * (g - g.mean(1, keepdims=True)) - c * (p * r * r / ((C - 1) * sd))
    return mxq(da, 0, "e5m2").T @ mxq(f64(o_attn).reshape(T, C), 0, "e4m3")

@@ -1,0 +1,261 @@
+from contextlib import ExitStack
+
+import concourse.mybir as mybir
+
+F32 = mybir.dt.float32
+BF16 = mybir.dt.bfloat16
+U32 = mybir.dt.uint32
+U8 = mybir.dt.uint8
+E4M3X4 = mybir.dt.float8_e4m3fn_x4
+E5M2X4 = mybir.dt.float8_e5m2_x4
+ALU = mybir.AluOpType
+ACT = mybir.ActivationFunctionType
+
+P = 128
+PACK = 4
+K_PASS = P * PACK
+GRID = 32
+WS = 8
+SHIFT = 4
+WINDOWS_ACROSS = GRID // WS
+WINDOW_ROWS = WS * WS
+ROWS = GRID * GRID
+C = 1024
+PASSES = ROWS // K_PASS
+EPS = 1e-5
+BN_WIDTH = 512
+N_TILE = 512
+M_TILES = C // P
+N_TILES = C // N_TILE
+BANKS = 8
+ROUND = BANKS // N_TILES
+PIECE = 256
+
+FLOPS = 2 * ROWS * C * C
+BYTES = ROWS * C * (2 + 2 + 4) + ROWS * 2 + C * C * 4
+
+
+def cyclic_runs(start, length, period):
+    first = start % period
+    head = min(length, period - first)
+    runs = [(0, first, head)]
+    if head < length:
+        runs.append((head, 0, length - head))
+    return runs
+
+
+def tile_swintransformerblock_pb_v_kernel(
+    tc, o_attn, out_w, out_b, ada1_scale, ada1_shift, x, a, grad_out, out
+):
+    nc = tc.nc
+    a_view = a.flatten_outer_dims().rearrange("(h p t) c -> h p t c", h=PASSES, p=P)
+    o_view = o_attn.flatten_outer_dims().rearrange("(h p t) c -> h p (t c)", h=PASSES, p=P)
+    grad_grid = grad_out.rearrange("b (i j) c -> (b i) j c", j=GRID)
+    gain_grid = ada1_scale.rearrange("b (i j) o -> (b i) (j o)", j=GRID)
+
+    with ExitStack() as ctx:
+        keep = ctx.enter_context(tc.tile_pool(name="keep", bufs=1))
+        small = ctx.enter_context(tc.tile_pool(name="small", bufs=PASSES))
+        scratch = ctx.enter_context(tc.tile_pool(name="scratch", bufs=2))
+        stage = ctx.enter_context(tc.tile_pool(name="stage", bufs=M_TILES))
+        psum = ctx.enter_context(tc.psum_pool(name="psum", bufs=BANKS))
+        ctx.enter_context(tc.manual_schedule())
+
+        a_sb = keep.tile([P, PASSES, PACK, C], F32)
+        g_sb = keep.tile([P, PASSES, PACK, C], BF16)
+        o_rows = keep.tile([P, PASSES, PACK, C], BF16)
+        w_sb = keep.tile([P, PASSES, PACK, C], F32)
+        da_rows = keep.tile([P, PASSES, PACK, C], BF16)
+        da_grouped = keep.tile([P, PASSES, C, PACK], BF16, align_bytes=64)
+        o_grouped = keep.tile([P, PASSES, C, PACK], BF16, align_bytes=64)
+        da_codes = keep.tile([P, PASSES, C], U32, align_bytes=64)
+        da_scales = keep.tile([P, PASSES, C], U8, align_bytes=64)
+        o_codes = keep.tile([P, PASSES, C], U32, align_bytes=64)
+        o_scales = keep.tile([P, PASSES, C], U8, align_bytes=64)
+
+        def load_a(h):
+            for t in range(PACK):
+                nc.sync.dma_start(out=a_sb[:, h, t, :], in_=a_view[h, :, t, :])
+
+        def window_pieces(h):
+            pieces = []
+            for w in range(K_PASS // WINDOW_ROWS):
+                wi, wj = divmod(h * (K_PASS // WINDOW_ROWS) + w, WINDOWS_ACROSS)
+                base = w * (WINDOW_ROWS // PACK)
+                for r0, i0, n_rows in cyclic_runs(WS * wi + SHIFT, WS, GRID):
+                    for c0, j0, n_cols in cyclic_runs(WS * wj + SHIFT, WS, GRID):
+                        parts = slice(base + 2 * r0 + c0 // PACK, base + 2 * (r0 + n_rows), WS // n_cols)
+                        pieces.append((parts, slice(i0, i0 + n_rows), slice(j0, j0 + n_cols)))
+            return pieces
+
+        def load_grad(h, even_queue):
+            queues = [even_queue, nc.gpsimd]
+            for k, (parts, grid_rows, grid_cols) in enumerate(window_pieces(h)):
+                queues[k % 2].dma_start(
+                    out=g_sb[parts, h].rearrange("p t c -> p (t c)"),
+                    in_=grad_grid[grid_rows, grid_cols, :].rearrange("i j c -> i (j c)"),
+                )
+
+        def load_gain(h):
+            gain = small.tile([P, PACK], BF16)
+            for parts, grid_rows, grid_cols in window_pieces(h):
+                nc.sync.dma_start(out=gain[parts, :], in_=gain_grid[grid_rows, grid_cols])
+            return gain
+
+        def load_o(h):
+            nc.sync.dma_start(out=o_rows[:, h].rearrange("p t c -> p (t c)"), in_=o_view[h])
+
+        def regroup(copy, grouped, rows, cols):
+            copy(
+                out=grouped[:, cols, :].rearrange("p (c i) t -> p c t i", i=4),
+                in_=rows[:, :, cols].rearrange("p t (c i) -> p c t i", i=4),
+            )
+
+        def quantise(codes, scales, grouped, x4, cols):
+            nc.vector.quantize_mx(
+                out=codes[:, cols].bitcast(x4),
+                scales=scales[:, cols],
+                in_=grouped[:, cols, :].rearrange("p c t -> p (c t)"),
+            )
+
+        def row_statistics(h):
+            stats = small.tile([P, PACK, C // BN_WIDTH, 6], F32)
+            mean_var = small.tile([P, PACK, 2], F32)
+            for t in range(PACK):
+                for b in range(C // BN_WIDTH):
+                    nc.vector.bn_stats(out=stats[:, t, b, :], in_=a_sb[:, h, t, b * BN_WIDTH : (b + 1) * BN_WIDTH])
+            for t in range(PACK):
+                nc.vector.bn_aggr(out=mean_var[:, t, :], in_=stats[:, t].rearrange("p b s -> p (b s)"))
+            sd = small.tile([P, PACK], F32)
+            nc.scalar.activation(out=sd[:], in_=mean_var[:, :, 1], func=ACT.Sqrt, scale=C / (C - 1))
+            return mean_var, sd
+
+        def row_coefficients(h, mean_var, sd, gain):
+            p_sum = small.tile([P, PACK], F32)
+            sd_eps = small.tile([P, PACK], F32)
+            r = small.tile([P, PACK], F32)
+            denom = small.tile([P, PACK], F32)
+            inv_denom = small.tile([P, PACK], F32)
+            alpha = small.tile([P, PACK], F32)
+            minus_alpha_over_c = small.tile([P, PACK], F32)
+            kappa = small.tile([P, PACK], F32)
+
+            def product(t):
+                unused = scratch.tile([P, C], BF16)
+                nc.vector.scalar_tensor_tensor(
+                    out=unused[:],
+                    in0=a_sb[:, h, t, :],
+                    scalar=mean_var[:, t, 0:1],
+                    in1=g_sb[:, h, t, :],
+                    op0=ALU.subtract,
+                    op1=ALU.mult,
+                    accum_out=p_sum[:, t : t + 1],
+                )
+
+            product(0)
+            nc.vector.tensor_scalar_add(out=sd_eps[:], in0=sd[:], scalar1=EPS)
+            product(1)
+            nc.vector.reciprocal(out=r[:], in_=sd_eps[:])
+            nc.vector.tensor_mul(out=denom[:], in0=sd_eps[:], in1=sd[:])
+            product(2)
+            nc.vector.reciprocal(out=inv_denom[:], in_=denom[:])
+            product(3)
+            nc.vector.tensor_mul(out=alpha[:], in0=r[:], in1=gain[:])
+            nc.vector.tensor_scalar_mul(out=minus_alpha_over_c[:], in0=alpha[:], scalar1=-1.0 / C)
+            nc.vector.scalar_tensor_tensor(
+                out=kappa[:], in0=p_sum[:], scalar=-1.0 / (C - 1), in1=inv_denom[:], op0=ALU.mult, op1=ALU.mult
+            )
+            return alpha, minus_alpha_over_c, kappa
+
+        def rows_of_da(h, alpha, minus_alpha_over_c, kappa):
+            w_sum = small.tile([P, PACK], F32)
+            beta = small.tile([P, PACK], F32)
+
+            def finish(t):
+                one = slice(t, t + 1)
+                nc.vector.tensor_mul(out=beta[:, one], in0=w_sum[:, one], in1=minus_alpha_over_c[:, one])
+                nc.scalar.activation(
+                    out=da_rows[:, h, t, :],
+                    in_=w_sb[:, h, t, :],
+                    func=ACT.Identity,
+                    scale=alpha[:, one],
+                    bias=beta[:, one],
+                )
+
+            for t in range(PACK):
+                nc.vector.scalar_tensor_tensor(
+                    out=w_sb[:, h, t, :],
+                    in0=a_sb[:, h, t, :],
+                    scalar=kappa[:, t : t + 1],
+                    in1=g_sb[:, h, t, :],
+                    op0=ALU.mult,
+                    op1=ALU.add,
+                    accum_out=w_sum[:, t : t + 1],
+                )
+                if t > 0:
+                    finish(t - 1)
+            finish(PACK - 1)
+
+        accs = {}
+
+        def multiply(h, m):
+            for n in range(N_TILES):
+                if h == 0:
+                    acc = psum.tile([P, N_TILE], F32)
+                    accs[(m, n)] = acc
+                nc.tensor.matmul_mx(
+                    out=accs[(m, n)][:],
+                    lhsT=da_codes[:, h, m * P : (m + 1) * P].bitcast(E5M2X4),
+                    lhsT_scale=da_scales[:, h, m * P : (m + 1) * P],
+                    rhs=o_codes[:, h, n * N_TILE : (n + 1) * N_TILE].bitcast(E4M3X4),
+                    rhs_scale=o_scales[:, h, n * N_TILE : (n + 1) * N_TILE],
+                    start=(h == 0),
+                    stop=(h == PASSES - 1),
+                )
+
+        def store(m):
+            result = stage.tile([P, C], F32)
+            nc.vector.tensor_copy(out=result[:, 0:N_TILE], in_=accs[(m, 0)][:])
+            nc.scalar.copy(out=result[:, N_TILE:C], in_=accs[(m, 1)][:])
+            nc.sync.dma_start(out=out[m * P : (m + 1) * P, :], in_=result[:])
+
+        whole = slice(0, C)
+        pieces = [slice(k * PIECE, (k + 1) * PIECE) for k in range(C // PIECE)]
+
+        load_a(0)
+        load_grad(0, nc.scalar)
+        gains = [load_gain(0)]
+        load_o(0)
+        load_a(1)
+        load_o(1)
+        load_grad(1, nc.sync)
+        gains.append(load_gain(1))
+
+        mean_var, sd = row_statistics(0)
+        alpha, minus_alpha_over_c, kappa = row_coefficients(0, mean_var, sd, gains[0])
+        for h in range(PASSES):
+            regroup(nc.scalar.copy, o_grouped[:, h], o_rows[:, h], whole)
+        mean_var, sd = row_statistics(1)
+        rows_of_da(0, alpha, minus_alpha_over_c, kappa)
+
+        quantise(o_codes[:, 0], o_scales[:, 0], o_grouped[:, 0], E4M3X4, whole)
+        alpha, minus_alpha_over_c, kappa = row_coefficients(1, mean_var, sd, gains[1])
+        regroup(nc.scalar.copy, da_grouped[:, 0], da_rows[:, 0], whole)
+        rows_of_da(1, alpha, minus_alpha_over_c, kappa)
+        quantise(da_codes[:, 0], da_scales[:, 0], da_grouped[:, 0], E5M2X4, whole)
+        for m in range(ROUND):
+            multiply(0, m)
+        quantise(o_codes[:, 1], o_scales[:, 1], o_grouped[:, 1], E4M3X4, whole)
+
+        copies = [nc.vector.tensor_copy, nc.scalar.copy]
+        for k, cols in enumerate(pieces):
+            regroup(copies[k % 2], da_grouped[:, 1], da_rows[:, 1], cols)
+        for cols in pieces:
+            quantise(da_codes[:, 1], da_scales[:, 1], da_grouped[:, 1], E5M2X4, cols)
+        for m in range(ROUND):
+            multiply(1, m)
+        for m in range(M_TILES):
+            store(m)
+            if m + ROUND < M_TILES:
+                for h in range(PASSES):
+                    multiply(h, m + ROUND)

@@ -48,8 +48,8 @@ def tile_swintransformerblock_pb_v_kernel(
     tc, o_attn, out_w, out_b, ada1_scale, ada1_shift, x, a, grad_out, out
 ):
     nc = tc.nc
-    a_view = a.flatten_outer_dims().rearrange("(h p t) c -> h p t c", h=PASSES, p=P)
-    o_view = o_attn.flatten_outer_dims().rearrange("(h p t) c -> h p (t c)", h=PASSES, p=P)
+    a_view = a.flatten_outer_dims().rearrange("(h w n t) c -> h t n w c", h=PASSES, w=2, t=PACK)
+    o_view = o_attn.flatten_outer_dims().rearrange("(h w n t) c -> h n w (t c)", h=PASSES, w=2, t=PACK)
     grad_grid = grad_out.rearrange("b (i j) c -> (b i) j c", j=GRID)
     gain_grid = ada1_scale.rearrange("b (i j) o -> (b i) (j o)", j=GRID)
 
@@ -75,16 +75,19 @@ def tile_swintransformerblock_pb_v_kernel(
 
         def load_a(h):
             for t in range(PACK):
-                nc.sync.dma_start(out=a_sb[:, h, t, :], in_=a_view[h, :, t, :])
+                nc.sync.dma_start(out=a_sb[:, h, t, :], in_=a_view[h, t])
 
         def window_pieces(h):
             pieces = []
             for w in range(K_PASS // WINDOW_ROWS):
                 wi, wj = divmod(h * (K_PASS // WINDOW_ROWS) + w, WINDOWS_ACROSS)
-                base = w * (WINDOW_ROWS // PACK)
+                base = 2 * wj * (WINDOW_ROWS // PACK) + wi % 2
                 for r0, i0, n_rows in cyclic_runs(WS * wi + SHIFT, WS, GRID):
                     for c0, j0, n_cols in cyclic_runs(WS * wj + SHIFT, WS, GRID):
-                        parts = slice(base + 2 * r0 + c0 // PACK, base + 2 * (r0 + n_rows), WS // n_cols)
+                        first = base + 2 * (2 * r0 + c0 // PACK)
+                        step = 2 * (WS // n_cols)
+                        count = n_rows * n_cols // PACK
+                        parts = slice(first, first + step * (count - 1) + 1, step)
                         pieces.append((parts, slice(i0, i0 + n_rows), slice(j0, j0 + n_cols)))
             return pieces
 

from contextlib import ExitStack

import concourse.mybir as mybir

F32 = mybir.dt.float32
BF16 = mybir.dt.bfloat16
U32 = mybir.dt.uint32
U8 = mybir.dt.uint8
E4M3X4 = mybir.dt.float8_e4m3fn_x4
E5M2X4 = mybir.dt.float8_e5m2_x4
ALU = mybir.AluOpType
ACT = mybir.ActivationFunctionType

P = 128
PACK = 4
K_PASS = P * PACK
GRID = 32
WS = 8
SHIFT = 4
WINDOWS_ACROSS = GRID // WS
WINDOW_ROWS = WS * WS
ROWS = GRID * GRID
C = 1024
PASSES = ROWS // K_PASS
EPS = 1e-5
BN_WIDTH = 512
N_TILE = 512
M_TILES = C // P
N_TILES = C // N_TILE
BANKS = 8
ROUND = BANKS // N_TILES
PIECE = 256

FLOPS = 2 * ROWS * C * C
BYTES = ROWS * C * (2 + 2 + 4) + ROWS * 2 + C * C * 4


def cyclic_runs(start, length, period):
    first = start % period
    head = min(length, period - first)
    runs = [(0, first, head)]
    if head < length:
        runs.append((head, 0, length - head))
    return runs


def tile_swintransformerblock_pb_v_kernel(
    tc, o_attn, out_w, out_b, ada1_scale, ada1_shift, x, a, grad_out, out
):
    nc = tc.nc
    a_view = a.flatten_outer_dims().rearrange("(h w n t) c -> h t n w c", h=PASSES, w=2, t=PACK)
    o_view = o_attn.flatten_outer_dims().rearrange("(h w n t) c -> h n w (t c)", h=PASSES, w=2, t=PACK)
    grad_grid = grad_out.rearrange("b (i j) c -> (b i) j c", j=GRID)
    gain_grid = ada1_scale.rearrange("b (i j) o -> (b i) (j o)", j=GRID)

    with ExitStack() as ctx:
        keep = ctx.enter_context(tc.tile_pool(name="keep", bufs=1))
        small = ctx.enter_context(tc.tile_pool(name="small", bufs=PASSES))
        scratch = ctx.enter_context(tc.tile_pool(name="scratch", bufs=2))
        stage = ctx.enter_context(tc.tile_pool(name="stage", bufs=M_TILES))
        psum = ctx.enter_context(tc.psum_pool(name="psum", bufs=BANKS))
        ctx.enter_context(tc.manual_schedule())

        a_sb = keep.tile([P, PASSES, PACK, C], F32)
        g_sb = keep.tile([P, PASSES, PACK, C], BF16)
        o_rows = keep.tile([P, PASSES, PACK, C], BF16)
        w_sb = keep.tile([P, PASSES, PACK, C], F32)
        da_rows = keep.tile([P, PASSES, PACK, C], BF16)
        da_grouped = keep.tile([P, PASSES, C, PACK], BF16, align_bytes=64)
        o_grouped = keep.tile([P, PASSES, C, PACK], BF16, align_bytes=64)
        da_codes = keep.tile([P, PASSES, C], U32, align_bytes=64)
        da_scales = keep.tile([P, PASSES, C], U8, align_bytes=64)
        o_codes = keep.tile([P, PASSES, C], U32, align_bytes=64)
        o_scales = keep.tile([P, PASSES, C], U8, align_bytes=64)

        def load_a(h):
            for t in range(PACK):
                nc.sync.dma_start(out=a_sb[:, h, t, :], in_=a_view[h, t])

        def window_pieces(h):
            pieces = []
            for w in range(K_PASS // WINDOW_ROWS):
                wi, wj = divmod(h * (K_PASS // WINDOW_ROWS) + w, WINDOWS_ACROSS)
                base = 2 * wj * (WINDOW_ROWS // PACK) + wi % 2
                for r0, i0, n_rows in cyclic_runs(WS * wi + SHIFT, WS, GRID):
                    for c0, j0, n_cols in cyclic_runs(WS * wj + SHIFT, WS, GRID):
                        first = base + 2 * (2 * r0 + c0 // PACK)
                        step = 2 * (WS // n_cols)
                        count = n_rows * n_cols // PACK
                        parts = slice(first, first + step * (count - 1) + 1, step)
                        pieces.append((parts, slice(i0, i0 + n_rows), slice(j0, j0 + n_cols)))
            return pieces

        def load_grad(h, even_queue):
            queues = [even_queue, nc.gpsimd]
            for k, (parts, grid_rows, grid_cols) in enumerate(window_pieces(h)):
                queues[k % 2].dma_start(
                    out=g_sb[parts, h].rearrange("p t c -> p (t c)"),
                    in_=grad_grid[grid_rows, grid_cols, :].rearrange("i j c -> i (j c)"),
                )

        def load_gain(h):
            gain = small.tile([P, PACK], BF16)
            for parts, grid_rows, grid_cols in window_pieces(h):
                nc.sync.dma_start(out=gain[parts, :], in_=gain_grid[grid_rows, grid_cols])
            return gain

        def load_o(h):
            nc.sync.dma_start(out=o_rows[:, h].rearrange("p t c -> p (t c)"), in_=o_view[h])

        def regroup(copy, grouped, rows, cols):
            copy(
                out=grouped[:, cols, :].rearrange("p (c i) t -> p c t i", i=4),
                in_=rows[:, :, cols].rearrange("p t (c i) -> p c t i", i=4),
            )

        def quantise(codes, scales, grouped, x4, cols):
            nc.vector.quantize_mx(
                out=codes[:, cols].bitcast(x4),
                scales=scales[:, cols],
                in_=grouped[:, cols, :].rearrange("p c t -> p (c t)"),
            )

        def row_statistics(h):
            stats = small.tile([P, PACK, C // BN_WIDTH, 6], F32)
            mean_var = small.tile([P, PACK, 2], F32)
            for t in range(PACK):
                for b in range(C // BN_WIDTH):
                    nc.vector.bn_stats(out=stats[:, t, b, :], in_=a_sb[:, h, t, b * BN_WIDTH : (b + 1) * BN_WIDTH])
            for t in range(PACK):
                nc.vector.bn_aggr(out=mean_var[:, t, :], in_=stats[:, t].rearrange("p b s -> p (b s)"))
            sd = small.tile([P, PACK], F32)
            nc.scalar.activation(out=sd[:], in_=mean_var[:, :, 1], func=ACT.Sqrt, scale=C / (C - 1))
            return mean_var, sd

        def row_coefficients(h, mean_var, sd, gain):
            p_sum = small.tile([P, PACK], F32)
            sd_eps = small.tile([P, PACK], F32)
            r = small.tile([P, PACK], F32)
            denom = small.tile([P, PACK], F32)
            inv_denom = small.tile([P, PACK], F32)
            alpha = small.tile([P, PACK], F32)
            minus_alpha_over_c = small.tile([P, PACK], F32)
            kappa = small.tile([P, PACK], F32)

            def product(t):
                unused = scratch.tile([P, C], BF16)
                nc.vector.scalar_tensor_tensor(
                    out=unused[:],
                    in0=a_sb[:, h, t, :],
                    scalar=mean_var[:, t, 0:1],
                    in1=g_sb[:, h, t, :],
                    op0=ALU.subtract,
                    op1=ALU.mult,
                    accum_out=p_sum[:, t : t + 1],
                )

            product(0)
            nc.vector.tensor_scalar_add(out=sd_eps[:], in0=sd[:], scalar1=EPS)
            product(1)
            nc.vector.reciprocal(out=r[:], in_=sd_eps[:])
            nc.vector.tensor_mul(out=denom[:], in0=sd_eps[:], in1=sd[:])
            product(2)
            nc.vector.reciprocal(out=inv_denom[:], in_=denom[:])
            product(3)
            nc.vector.tensor_mul(out=alpha[:], in0=r[:], in1=gain[:])
            nc.vector.tensor_scalar_mul(out=minus_alpha_over_c[:], in0=alpha[:], scalar1=-1.0 / C)
            nc.vector.scalar_tensor_tensor(
                out=kappa[:], in0=p_sum[:], scalar=-1.0 / (C - 1), in1=inv_denom[:], op0=ALU.mult, op1=ALU.mult
            )
            return alpha, minus_alpha_over_c, kappa

        def rows_of_da(h, alpha, minus_alpha_over_c, kappa):
            w_sum = small.tile([P, PACK], F32)
            beta = small.tile([P, PACK], F32)

            def finish(t):
                one = slice(t, t + 1)
                nc.vector.tensor_mul(out=beta[:, one], in0=w_sum[:, one], in1=minus_alpha_over_c[:, one])
                nc.scalar.activation(
                    out=da_rows[:, h, t, :],
                    in_=w_sb[:, h, t, :],
                    func=ACT.Identity,
                    scale=alpha[:, one],
                    bias=beta[:, one],
                )

            for t in range(PACK):
                nc.vector.scalar_tensor_tensor(
                    out=w_sb[:, h, t, :],
                    in0=a_sb[:, h, t, :],
                    scalar=kappa[:, t : t + 1],
                    in1=g_sb[:, h, t, :],
                    op0=ALU.mult,
                    op1=ALU.add,
                    accum_out=w_sum[:, t : t + 1],
                )
                if t > 0:
                    finish(t - 1)
            finish(PACK - 1)

        accs = {}

        def multiply(h, m):
            for n in range(N_TILES):
                if h == 0:
                    acc = psum.tile([P, N_TILE], F32)
                    accs[(m, n)] = acc
                nc.tensor.matmul_mx(
                    out=accs[(m, n)][:],
                    lhsT=da_codes[:, h, m * P : (m + 1) * P].bitcast(E5M2X4),
                    lhsT_scale=da_scales[:, h, m * P : (m + 1) * P],
                    rhs=o_codes[:, h, n * N_TILE : (n + 1) * N_TILE].bitcast(E4M3X4),
                    rhs_scale=o_scales[:, h, n * N_TILE : (n + 1) * N_TILE],
                    start=(h == 0),
                    stop=(h == PASSES - 1),
                )

        def store(m):
            result = stage.tile([P, C], F32)
            nc.vector.tensor_copy(out=result[:, 0:N_TILE], in_=accs[(m, 0)][:])
            nc.scalar.copy(out=result[:, N_TILE:C], in_=accs[(m, 1)][:])
            nc.sync.dma_start(out=out[m * P : (m + 1) * P, :], in_=result[:])

        whole = slice(0, C)
        pieces = [slice(k * PIECE, (k + 1) * PIECE) for k in range(C // PIECE)]

        load_a(0)
        load_grad(0, nc.scalar)
        gains = [load_gain(0)]
        load_o(0)
        load_a(1)
        load_o(1)
        load_grad(1, nc.sync)
        gains.append(load_gain(1))

        mean_var, sd = row_statistics(0)
        alpha, minus_alpha_over_c, kappa = row_coefficients(0, mean_var, sd, gains[0])
        for h in range(PASSES):
            regroup(nc.scalar.copy, o_grouped[:, h], o_rows[:, h], whole)
        mean_var, sd = row_statistics(1)
        rows_of_da(0, alpha, minus_alpha_over_c, kappa)

        quantise(o_codes[:, 0], o_scales[:, 0], o_grouped[:, 0], E4M3X4, whole)
        alpha, minus_alpha_over_c, kappa = row_coefficients(1, mean_var, sd, gains[1])
        regroup(nc.scalar.copy, da_grouped[:, 0], da_rows[:, 0], whole)
        rows_of_da(1, alpha, minus_alpha_over_c, kappa)
        quantise(da_codes[:, 0], da_scales[:, 0], da_grouped[:, 0], E5M2X4, whole)
        for m in range(ROUND):
            multiply(0, m)
        quantise(o_codes[:, 1], o_scales[:, 1], o_grouped[:, 1], E4M3X4, whole)

        copies = [nc.vector.tensor_copy, nc.scalar.copy]
        for k, cols in enumerate(pieces):
            regroup(copies[k % 2], da_grouped[:, 1], da_rows[:, 1], cols)
        for cols in pieces:
            quantise(da_codes[:, 1], da_scales[:, 1], da_grouped[:, 1], E5M2X4, cols)
        for m in range(ROUND):
            multiply(1, m)
        for m in range(M_TILES):
            store(m)
            if m + ROUND < M_TILES:
                for h in range(PASSES):
                    multiply(h, m + ROUND)
